import numpy as np
import ml_dtypes


def mxq(x, axis, fmt="e4m3"):
    dtype, down = {"e4m3": (ml_dtypes.float8_e4m3fn, 7), "e5m2": (ml_dtypes.float8_e5m2, 14)}[fmt]
    v = np.moveaxis(np.asarray(x, np.float32).astype(ml_dtypes.bfloat16).astype(np.float64), axis, -1)
    blocks = v.reshape(v.shape[:-1] + (-1, 32))
    amax = np.abs(blocks).max(-1, keepdims=True)
    byte = np.maximum(np.where(amax > 0, np.frexp(amax)[1] - 1 + 127, 0) - down, 1)
    scale = np.exp2(byte - 127.0)
    codes = (blocks / scale).astype(np.float32).astype(dtype).astype(np.float64)
    return np.moveaxis((codes * scale).reshape(v.shape), -1, axis)


WIDE = False


def mx_kscale(k):
    if not WIDE:
        return np.ones(k)
    levels = np.array([10, -10, 5, -5, 0])
    a = np.random.permutation(np.resize(levels, k // 512 * 4)).reshape(k // 512, 4)
    idx = np.arange(k)
    return np.exp2(a[idx // 512, idx % 128 // 32])


BF16 = ml_dtypes.bfloat16


def bf(x):
    return np.asarray(x, np.float32).astype(BF16)


def f64(x):
    return np.asarray(x).astype(np.float64)


E2M1 = np.array([0.0, 0.5, 1.0, 1.5, 2.0, 3.0, 4.0, 6.0, -0.0, -0.5, -1.0, -1.5, -2.0, -3.0, -4.0, -6.0])


def pack_weight(w, fmt):
    k, n = w.shape
    w = f64(bf(w)).reshape(k // 32, 32, n)
    amax = np.abs(w).max(1)
    if fmt == "e4m3":
        byte = np.frexp(amax)[1] - 1 + 127 - 7
    else:
        mant, ex = np.frexp(amax / 6.0)
        byte = np.where(mant > 0.5, ex, ex - 1) + 127
    byte = np.clip(np.where(amax > 0, byte, 1), 1, 254)
    scaled = (w * np.exp2(127.0 - byte)[:, None, :]).reshape(k, n).astype(np.float32)
    by_word = np.ascontiguousarray(scaled.reshape(k // 512, 128, 4, n).transpose(0, 1, 3, 2))
    if fmt == "e4m3":
        words = by_word.astype(ml_dtypes.float8_e4m3fn).view(np.uint8)
    else:
        c = by_word.astype(ml_dtypes.float4_e2m1fn).view(np.uint8) & 0xF
        words = c[..., 0::2] | (c[..., 1::2] << 4)
    return np.ascontiguousarray(words), np.ascontiguousarray(byte.astype(np.uint8).reshape(k // 512, 16, n))


def unpack_weight(words, scales, fmt):
    g, p, n, _ = words.shape
    if fmt == "e4m3":
        vals = np.ascontiguousarray(words).view(ml_dtypes.float8_e4m3fn).astype(np.float64)
    else:
        nib = np.empty((g, p, n, 4), np.uint8)
        nib[..., 0::2] = words & 0xF
        nib[..., 1::2] = words >> 4
        vals = E2M1[nib]
    vals = vals * np.repeat(np.exp2(scales.astype(np.float64) - 127.0), 8, axis=1)[..., None]
    return vals.transpose(0, 1, 3, 2).reshape(g * 512, n)

def pack4(w):
    words, scales = pack_weight(w, "e2m1")
    return words.reshape(words.shape[0], 128, -1), scales


def unpack4(words, scales):
    return unpack_weight(words.reshape(words.shape[0], 128, -1, 2), scales, "e2m1")


B, CIN, H, W, CP, G = 4, 256, 32, 32, 2048, 2
CG = CP // G
CO = CIN // G
HW = H * W
EPS = 1e-5


def setup_inputs():
    s = mx_kscale(CG)
    y = bf((np.random.standard_normal((B, G, CG, HW)) * 2.5 + 1.0) * s[None, None, :, None])
    stack = ((np.random.standard_normal((G, CO, CG)) / np.sqrt(CG) + 1.5 / CG) / s).swapaxes(1, 2)
    words, scales = pack4(stack.reshape(-1, CO))
    return {"y": y,
            "Wz_words": words,
            "Wz_scales": scales,
            "gamma": bf(1.0 + 0.1 * np.random.standard_normal(CIN)),
            "beta": bf(0.1 * np.random.standard_normal(CIN)),
            "x": bf(np.random.standard_normal((B, CIN, H, W)))}


def reference(y, Wz_words, Wz_scales, gamma, beta, x):
    wq = unpack4(Wz_words, Wz_scales).reshape(G, CG, CO).swapaxes(1, 2)
    z = wq @ mxq(f64(y), 2, "e4m3")
    zr = z.reshape(B, G, CO * HW)
    mu = zr.mean(-1, keepdims=True)
    var = zr.var(-1, keepdims=True)
    zn = ((zr - mu) * (1.0 / np.sqrt(var + EPS))).reshape(B, CIN, H, W)
    return zn * f64(gamma)[None, :, None, None] + f64(beta)[None, :, None, None] + f64(x)

@@ -1,0 +1,238 @@
+from contextlib import ExitStack
+
+import concourse.mybir as mybir
+from concourse.masks import make_identity
+
+F32 = mybir.dt.float32
+BF16 = mybir.dt.bfloat16
+I32 = mybir.dt.int32
+U32 = mybir.dt.uint32
+U8 = mybir.dt.uint8
+FP8X4 = mybir.dt.float8_e4m3fn_x4
+FP4X4 = mybir.dt.float4_e2m1fn_x4
+ALU = mybir.AluOpType
+ACT = mybir.ActivationFunctionType
+
+P = 128
+PACK = 4
+K_PASS = P * PACK
+IMAGES, GROUPS, CHANNELS, POSITIONS = 4, 2, 1024, 1024
+UNITS = IMAGES * GROUPS
+PASSES = CHANNELS // K_PASS
+CHUNKS = UNITS * PASSES
+BANK = 512
+HALVES = POSITIONS // BANK
+EPS = 1e-5
+
+FLOPS = 2 * UNITS * P * CHANNELS * POSITIONS
+
+VECTOR_COLS = 384
+RUN = 4
+RAW_BUFS = 8
+
+
+def tile_spatialcgnl_pb_t_e_kernel(tc, y, Wz_words, Wz_scales, gamma, beta, x, out):
+    nc = tc.nc
+    y_chunks = y.rearrange("b j (c p t) n -> (b j c) p t n", c=PASSES, p=P, t=PACK)
+    x_images = x.rearrange("b (j o) h w -> b o j (h w)", j=GROUPS)
+    out_units = out.rearrange("b (j o) h w -> (b j) o (h w)", j=GROUPS)
+
+    with ExitStack() as ctx:
+        keep = ctx.enter_context(tc.tile_pool(name="keep", bufs=1))
+        raw_pool = ctx.enter_context(tc.tile_pool(name="raw", bufs=RAW_BUFS))
+        grouped_pool = ctx.enter_context(tc.tile_pool(name="grouped", bufs=3))
+        mx_pool = ctx.enter_context(tc.tile_pool(name="mx", bufs=3))
+        stat_pool = ctx.enter_context(tc.tile_pool(name="stat", bufs=4))
+        wide_pool = ctx.enter_context(tc.tile_pool(name="wide", bufs=3))
+        z_pool = ctx.enter_context(tc.psum_pool(name="z", bufs=3))
+        small_psum = ctx.enter_context(tc.psum_pool(name="small_psum", bufs=2))
+        ctx.enter_context(tc.manual_schedule())
+
+        w_words = keep.tile([P, GROUPS * PASSES, 2 * P], U8, align_bytes=64)
+        w_planes = keep.tile([P, GROUPS * PASSES, P], U8, align_bytes=64)
+        x_all = keep.tile([P, UNITS, POSITIONS], BF16)
+        affine_rows = keep.tile([P, P], BF16)
+        identity = keep.tile([P, P], BF16)
+        averager = keep.tile([P, P], F32)
+        gamma_beta = keep.tile([P, 2 * GROUPS], F32)
+        one = keep.tile([P, 1], F32)
+        table_warm = keep.tile([P, 1], F32)
+
+        raw = {}
+        grouped = {}
+        codes = {}
+        scales = {}
+        z = {}
+        moments = {}
+        totals = {}
+        rstd = {}
+        gain = {}
+        neg_shift = {}
+        neg_rest = {}
+
+        def load_chunk(i):
+            raw[i] = raw_pool.tile([P, PACK, POSITIONS], BF16, name="raw")
+            nc.sync.dma_start(out=raw[i][:], in_=y_chunks[i])
+            if i % (GROUPS * PASSES) == GROUPS * PASSES - 1:
+                b = i // (GROUPS * PASSES)
+                nc.sync.dma_start(out=x_all[:, GROUPS * b : GROUPS * (b + 1), :], in_=x_images[b])
+
+        def load_weights():
+            nc.sync.dma_start(
+                out=w_words[:].bitcast(I32), in_=Wz_words.bitcast(I32).rearrange("g p n -> p g n")
+            )
+            for quadrant in range(4):
+                nc.sync.dma_start(
+                    out=w_planes[32 * quadrant : 32 * quadrant + 4].bitcast(I32),
+                    in_=Wz_scales[:, 4 * quadrant : 4 * quadrant + 4, :]
+                    .bitcast(I32)
+                    .rearrange("g r n -> r g n"),
+                )
+
+        def regroup(i):
+            grouped[i] = grouped_pool.tile([P, POSITIONS, PACK], BF16, name="grouped", align_bytes=64)
+            for copy, cols in (
+                (nc.vector.tensor_copy, slice(0, VECTOR_COLS)),
+                (nc.scalar.copy, slice(VECTOR_COLS, POSITIONS)),
+            ):
+                copy(
+                    out=grouped[i][:, cols, :].rearrange("p (c r) t -> p c t r", r=RUN),
+                    in_=raw[i][:, :, cols].rearrange("p t (c r) -> p c t r", r=RUN),
+                )
+
+        def quantise_and_multiply(i):
+            unit, k_pass = divmod(i, PASSES)
+            slab = (unit % GROUPS) * PASSES + k_pass
+            codes[i] = mx_pool.tile([P, POSITIONS], U32, name="codes", align_bytes=64)
+            scales[i] = mx_pool.tile([P, POSITIONS], U8, name="scales", align_bytes=64)
+            nc.vector.quantize_mx(
+                out=codes[i][:].bitcast(FP8X4),
+                scales=scales[i][:],
+                in_=grouped[i][:].rearrange("p n t -> p (n t)"),
+            )
+            if k_pass == 0:
+                z[unit] = [z_pool.tile([P, BANK], F32, name="z%d" % h) for h in range(HALVES)]
+            for h in range(HALVES):
+                cols = slice(h * BANK, (h + 1) * BANK)
+                nc.tensor.matmul_mx(
+                    out=z[unit][h][:],
+                    lhsT=w_words[:, slab, :].bitcast(FP4X4),
+                    lhsT_scale=w_planes[:, slab, :],
+                    rhs=codes[i][:, cols].bitcast(FP8X4),
+                    rhs_scale=scales[i][:, cols],
+                    start=(k_pass == 0),
+                    stop=(k_pass == PASSES - 1),
+                )
+
+        def row_moments(unit):
+            parts = stat_pool.tile([P, HALVES, 6], F32, name="parts")
+            for h in range(HALVES):
+                nc.vector.bn_stats(out=parts[:, h, :], in_=z[unit][h][:])
+            moments[unit] = stat_pool.tile([P, 2], F32, name="moments")
+            nc.vector.bn_aggr(out=moments[unit][:], in_=parts[:].rearrange("p h s -> p (h s)"))
+            totals[unit] = small_psum.tile([P, 2], F32, name="totals", tag="small")
+            nc.tensor.matmul(
+                out=totals[unit][:, 0:1], lhsT=averager[:], rhs=moments[unit][:, 0:1], start=True, stop=True
+            )
+
+        def unit_variance(unit):
+            offset = stat_pool.tile([P, 1], F32, name="offset")
+            nc.vector.tensor_sub(out=offset[:], in0=moments[unit][:, 0:1], in1=totals[unit][:, 0:1])
+            spread = stat_pool.tile([P, 1], F32, name="spread")
+            nc.vector.scalar_tensor_tensor(
+                out=spread[:],
+                in0=offset[:],
+                scalar=offset[:, 0:1],
+                in1=moments[unit][:, 1:2],
+                op0=ALU.mult,
+                op1=ALU.add,
+            )
+            nc.tensor.matmul(out=totals[unit][:, 1:2], lhsT=averager[:], rhs=spread[:], start=True, stop=True)
+
+        def inverse_deviation(unit):
+            rstd[unit] = stat_pool.tile([P, 1], F32, name="rstd")
+            nc.scalar.activation(
+                out=rstd[unit][:], in_=totals[unit][:, 1:2], func=ACT.Abs_reciprocal_sqrt, bias=EPS, scale=1.0
+            )
+
+        def channel_affine(unit):
+            j = unit % GROUPS
+            gain[unit] = stat_pool.tile([P, 1], F32, name="gain")
+            nc.vector.tensor_mul(out=gain[unit][:], in0=rstd[unit][:], in1=gamma_beta[:, j : j + 1])
+            neg_shift[unit] = stat_pool.tile([P, 1], F32, name="neg_shift")
+            nc.vector.tensor_scalar(
+                out=neg_shift[unit][:],
+                in0=totals[unit][:, 0:1],
+                scalar1=gain[unit][:, 0:1],
+                scalar2=gamma_beta[:, GROUPS + j : GROUPS + j + 1],
+                op0=ALU.mult,
+                op1=ALU.subtract,
+            )
+
+        def shift_residual(unit):
+            neg_rest[unit] = wide_pool.tile([P, POSITIONS], F32, name="neg_rest")
+            nc.scalar.activation(
+                out=neg_rest[unit][:],
+                in_=x_all[:, unit, :],
+                func=ACT.Identity,
+                bias=neg_shift[unit][:, 0:1],
+                scale=-1.0,
+            )
+
+        def finish(unit):
+            result = wide_pool.tile([P, POSITIONS], F32, name="result")
+            for h in range(HALVES):
+                cols = slice(h * BANK, (h + 1) * BANK)
+                nc.vector.scalar_tensor_tensor(
+                    out=result[:, cols],
+                    in0=z[unit][h][:],
+                    scalar=gain[unit][:, 0:1],
+                    in1=neg_rest[unit][:, cols],
+                    op0=ALU.mult,
+                    op1=ALU.subtract,
+                )
+            nc.sync.dma_start(out=out_units[unit], in_=result[:])
+
+        nc.vector.memset(w_planes[:].rearrange("p g n -> p (g n)").bitcast(I32), 0)
+        nc.vector.memset(one[:], 1.0)
+        nc.scalar.activation(out=table_warm[:], in_=one[:], func=ACT.Abs_reciprocal_sqrt)
+        nc.gpsimd.memset(affine_rows[:], 0.0)
+        nc.gpsimd.dma_start(out=affine_rows[0:GROUPS, :], in_=gamma.rearrange("(j o) -> j o", j=GROUPS))
+        nc.gpsimd.dma_start(out=affine_rows[GROUPS : 2 * GROUPS, :], in_=beta.rearrange("(j o) -> j o", j=GROUPS))
+        make_identity(nc, identity[:])
+        nc.gpsimd.memset(averager[:], 1.0 / P)
+        load_chunk(0)
+        load_chunk(1)
+        load_weights()
+        for i in range(2, RAW_BUFS - 1):
+            load_chunk(i)
+
+        def unpack_affine_rows():
+            columns = small_psum.tile([P, P], BF16, name="columns", tag="small")
+            nc.tensor.transpose(out=columns[:], in_=affine_rows[:], identity=identity[:])
+            nc.vector.tensor_copy(out=gamma_beta[:], in_=columns[:, 0 : 2 * GROUPS])
+
+        def unit_at(step, distance):
+            unit, odd = divmod(step - distance, PASSES)
+            return unit if odd == 0 and 0 <= unit < UNITS else None
+
+        for step in range(CHUNKS + 5):
+            if step + RAW_BUFS - 1 < CHUNKS:
+                load_chunk(step + RAW_BUFS - 1)
+            if step < CHUNKS:
+                regroup(step)
+            if step == 1:
+                unpack_affine_rows()
+            if unit_at(step, 5) is not None:
+                channel_affine(unit_at(step, 5))
+                shift_residual(unit_at(step, 5))
+            if unit_at(step, 3) is not None:
+                row_moments(unit_at(step, 3))
+            if unit_at(step, 4) is not None:
+                inverse_deviation(unit_at(step, 4))
+            if 1 <= step <= CHUNKS:
+                quantise_and_multiply(step - 1)
+            if unit_at(step, 3) is not None:
+                unit_variance(unit_at(step, 3))
+            if unit_at(step, 6) is not None:
+                finish(unit_at(step, 6))

@@ -26,9 +26,11 @@ EPS = 1e-5
 
 FLOPS = 2 * UNITS * P * CHANNELS * POSITIONS
 
-VECTOR_COLS = 384
 RUN = 4
-RAW_BUFS = 8
+EARLY_CHUNKS = 4
+VECTOR_EARLY = 512
+VECTOR_STEADY = 336
+GPSIMD_COLS = 0
 
 
 def tile_spatialcgnl_pb_t_e_kernel(tc, y, Wz_words, Wz_scales, gamma, beta, x, out):
@@ -39,7 +41,7 @@ def tile_spatialcgnl_pb_t_e_kernel(tc, y, Wz_words, Wz_scales, gamma, beta, x, o
 
     with ExitStack() as ctx:
         keep = ctx.enter_context(tc.tile_pool(name="keep", bufs=1))
-        raw_pool = ctx.enter_context(tc.tile_pool(name="raw", bufs=RAW_BUFS))
+        raw_pool = ctx.enter_context(tc.tile_pool(name="raw", bufs=CHUNKS))
         grouped_pool = ctx.enter_context(tc.tile_pool(name="grouped", bufs=3))
         mx_pool = ctx.enter_context(tc.tile_pool(name="mx", bufs=3))
         stat_pool = ctx.enter_context(tc.tile_pool(name="stat", bufs=4))
@@ -70,6 +72,11 @@ def tile_spatialcgnl_pb_t_e_kernel(tc, y, Wz_words, Wz_scales, gamma, beta, x, o
         neg_shift = {}
         neg_rest = {}
 
+        def shares(i):
+            if i < EARLY_CHUNKS:
+                return VECTOR_EARLY, 0
+            return VECTOR_STEADY, 0
+
         def load_chunk(i):
             raw[i] = raw_pool.tile([P, PACK, POSITIONS], BF16, name="raw")
             nc.sync.dma_start(out=raw[i][:], in_=y_chunks[i])
@@ -89,16 +96,24 @@ def tile_spatialcgnl_pb_t_e_kernel(tc, y, Wz_words, Wz_scales, gamma, beta, x, o
                     .rearrange("g r n -> r g n"),
                 )
 
-        def regroup(i):
-            grouped[i] = grouped_pool.tile([P, POSITIONS, PACK], BF16, name="grouped", align_bytes=64)
-            for copy, cols in (
-                (nc.vector.tensor_copy, slice(0, VECTOR_COLS)),
-                (nc.scalar.copy, slice(VECTOR_COLS, POSITIONS)),
-            ):
-                copy(
-                    out=grouped[i][:, cols, :].rearrange("p (c r) t -> p c t r", r=RUN),
-                    in_=raw[i][:, :, cols].rearrange("p t (c r) -> p c t r", r=RUN),
-                )
+        def grouped_tile(i):
+            if i not in grouped:
+                grouped[i] = grouped_pool.tile([P, POSITIONS, PACK], BF16, name="grouped", align_bytes=64)
+            return grouped[i]
+
+        def regroup(copy, i, cols):
+            copy(
+                out=grouped_tile(i)[:, cols, :].rearrange("p (c r) t -> p c t r", r=RUN),
+                in_=raw[i][:, :, cols].rearrange("p t (c r) -> p c t r", r=RUN),
+            )
+
+        def regroup_vector(i):
+            regroup(nc.vector.tensor_copy, i, slice(0, shares(i)[0]))
+
+        def regroup_scalar(i, piece):
+            first = sum(shares(i))
+            middle = first + (POSITIONS - first) // 16 * 8
+            regroup(nc.scalar.copy, i, (slice(first, middle), slice(middle, POSITIONS))[piece])
 
         def quantise_and_multiply(i):
             unit, k_pass = divmod(i, PASSES)
@@ -136,18 +151,14 @@ def tile_spatialcgnl_pb_t_e_kernel(tc, y, Wz_words, Wz_scales, gamma, beta, x, o
             )
 
         def unit_variance(unit):
-            offset = stat_pool.tile([P, 1], F32, name="offset")
-            nc.vector.tensor_sub(out=offset[:], in0=moments[unit][:, 0:1], in1=totals[unit][:, 0:1])
-            spread = stat_pool.tile([P, 1], F32, name="spread")
-            nc.vector.scalar_tensor_tensor(
-                out=spread[:],
-                in0=offset[:],
-                scalar=offset[:, 0:1],
-                in1=moments[unit][:, 1:2],
-                op0=ALU.mult,
-                op1=ALU.add,
+            square = stat_pool.tile([P, 1], F32, name="square")
+            nc.scalar.activation(
+                out=square[:], in_=totals[unit][:, 0:1], func=ACT.Square, bias=moments[unit][:, 0:1], scale=-1.0
             )
-            nc.tensor.matmul(out=totals[unit][:, 1:2], lhsT=averager[:], rhs=spread[:], start=True, stop=True)
+            nc.tensor.matmul(out=totals[unit][:, 1:2], lhsT=averager[:], rhs=square[:], start=True, stop=False)
+            nc.tensor.matmul(
+                out=totals[unit][:, 1:2], lhsT=averager[:], rhs=moments[unit][:, 1:2], start=False, stop=True
+            )
 
         def inverse_deviation(unit):
             rstd[unit] = stat_pool.tile([P, 1], F32, name="rstd")
@@ -155,10 +166,13 @@ def tile_spatialcgnl_pb_t_e_kernel(tc, y, Wz_words, Wz_scales, gamma, beta, x, o
                 out=rstd[unit][:], in_=totals[unit][:, 1:2], func=ACT.Abs_reciprocal_sqrt, bias=EPS, scale=1.0
             )
 
-        def channel_affine(unit):
+        def channel_gain(unit):
             j = unit % GROUPS
             gain[unit] = stat_pool.tile([P, 1], F32, name="gain")
             nc.vector.tensor_mul(out=gain[unit][:], in0=rstd[unit][:], in1=gamma_beta[:, j : j + 1])
+
+        def channel_shift(unit):
+            j = unit % GROUPS
             neg_shift[unit] = stat_pool.tile([P, 1], F32, name="neg_shift")
             nc.vector.tensor_scalar(
                 out=neg_shift[unit][:],
@@ -171,12 +185,13 @@ def tile_spatialcgnl_pb_t_e_kernel(tc, y, Wz_words, Wz_scales, gamma, beta, x, o
 
         def shift_residual(unit):
             neg_rest[unit] = wide_pool.tile([P, POSITIONS], F32, name="neg_rest")
-            nc.scalar.activation(
+            nc.gpsimd.tensor_scalar(
                 out=neg_rest[unit][:],
-                in_=x_all[:, unit, :],
-                func=ACT.Identity,
-                bias=neg_shift[unit][:, 0:1],
-                scale=-1.0,
+                in0=x_all[:, unit, :],
+                scalar1=-1.0,
+                scalar2=neg_shift[unit][:, 0:1],
+                op0=ALU.mult,
+                op1=ALU.add,
             )
 
         def finish(unit):
@@ -193,46 +208,56 @@ def tile_spatialcgnl_pb_t_e_kernel(tc, y, Wz_words, Wz_scales, gamma, beta, x, o
                 )
             nc.sync.dma_start(out=out_units[unit], in_=result[:])
 
-        nc.vector.memset(w_planes[:].rearrange("p g n -> p (g n)").bitcast(I32), 0)
-        nc.vector.memset(one[:], 1.0)
-        nc.scalar.activation(out=table_warm[:], in_=one[:], func=ACT.Abs_reciprocal_sqrt)
-        nc.gpsimd.memset(affine_rows[:], 0.0)
-        nc.gpsimd.dma_start(out=affine_rows[0:GROUPS, :], in_=gamma.rearrange("(j o) -> j o", j=GROUPS))
-        nc.gpsimd.dma_start(out=affine_rows[GROUPS : 2 * GROUPS, :], in_=beta.rearrange("(j o) -> j o", j=GROUPS))
-        make_identity(nc, identity[:])
-        nc.gpsimd.memset(averager[:], 1.0 / P)
-        load_chunk(0)
-        load_chunk(1)
-        load_weights()
-        for i in range(2, RAW_BUFS - 1):
-            load_chunk(i)
-
         def unpack_affine_rows():
             columns = small_psum.tile([P, P], BF16, name="columns", tag="small")
             nc.tensor.transpose(out=columns[:], in_=affine_rows[:], identity=identity[:])
             nc.vector.tensor_copy(out=gamma_beta[:], in_=columns[:, 0 : 2 * GROUPS])
 
-        def unit_at(step, distance):
-            unit, odd = divmod(step - distance, PASSES)
-            return unit if odd == 0 and 0 <= unit < UNITS else None
+        nc.vector.memset(w_planes[:].rearrange("p g n -> p (g n)").bitcast(I32), 0)
+        nc.vector.memset(affine_rows[:], 0.0)
+        nc.vector.memset(one[:], 1.0)
+        nc.vector.memset(averager[:], 1.0 / P)
+        nc.scalar.dma_start(out=affine_rows[0:GROUPS, :], in_=gamma.rearrange("(j o) -> j o", j=GROUPS))
+        nc.scalar.dma_start(out=affine_rows[GROUPS : 2 * GROUPS, :], in_=beta.rearrange("(j o) -> j o", j=GROUPS))
+        nc.scalar.activation(out=table_warm[:], in_=one[:], func=ACT.Abs_reciprocal_sqrt)
+        make_identity(nc, identity[:])
+        load_chunk(0)
+        load_chunk(1)
+        load_weights()
+        for i in range(2, CHUNKS):
+            load_chunk(i)
 
-        for step in range(CHUNKS + 5):
-            if step + RAW_BUFS - 1 < CHUNKS:
-                load_chunk(step + RAW_BUFS - 1)
+        for i in range(2):
+            regroup_vector(i)
+            regroup_scalar(i, 0)
+            regroup_scalar(i, 1)
+
+        for step in range(CHUNKS + 3):
+            odd = step % 2 == 1
+            measured = (step - 1) // 2 if odd and step < CHUNKS else None
+            scaled = (step - 3) // 2 if odd and step >= 3 else None
+            finished = (step - 4) // 2 if not odd and step >= 4 else None
+            ahead = step + 2 if step + 2 < CHUNKS else None
             if step < CHUNKS:
-                regroup(step)
+                quantise_and_multiply(step)
+            if scaled is not None:
+                channel_gain(scaled)
+            if ahead is not None:
+                regroup_vector(ahead)
             if step == 1:
                 unpack_affine_rows()
-            if unit_at(step, 5) is not None:
-                channel_affine(unit_at(step, 5))
-                shift_residual(unit_at(step, 5))
-            if unit_at(step, 3) is not None:
-                row_moments(unit_at(step, 3))
-            if unit_at(step, 4) is not None:
-                inverse_deviation(unit_at(step, 4))
-            if 1 <= step <= CHUNKS:
-                quantise_and_multiply(step - 1)
-            if unit_at(step, 3) is not None:
-                unit_variance(unit_at(step, 3))
-            if unit_at(step, 6) is not None:
-                finish(unit_at(step, 6))
+            if scaled is not None:
+                channel_shift(scaled)
+                shift_residual(scaled)
+            if measured is not None:
+                row_moments(measured)
+            if finished is not None:
+                finish(finished)
+            if ahead is not None:
+                regroup_scalar(ahead, 0)
+            if measured is not None:
+                unit_variance(measured)
+            if ahead is not None:
+                regroup_scalar(ahead, 1)
+            if measured is not None:
+                inverse_deviation(measured)

@@ -108,7 +108,8 @@ def tile_spatialcgnl_pb_t_e_kernel(tc, y, Wz_words, Wz_scales, gamma, beta, x, o
             )
 
         def regroup_vector(i):
-            regroup(nc.vector.tensor_copy, i, slice(0, shares(i)[0]))
+            cols = slice(0, shares(i)[0])
+            nc.vector.tensor_copy(out=grouped_tile(i)[:, cols, :], in_=raw[i][:, :, cols].rearrange("p t n -> p n t"))
 
         def regroup_scalar(i, piece):
             first = sum(shares(i))

@@ -28,8 +28,8 @@ FLOPS = 2 * UNITS * P * CHANNELS * POSITIONS
 
 RUN = 4
 EARLY_CHUNKS = 4
-VECTOR_EARLY = 512
-VECTOR_STEADY = 336
+VECTOR_EARLY = 448
+VECTOR_STEADY = 272
 GPSIMD_COLS = 0
 
 

@@ -29,8 +29,12 @@ FLOPS = 2 * UNITS * P * CHANNELS * POSITIONS
 RUN = 4
 EARLY_CHUNKS = 4
 VECTOR_EARLY = 448
-VECTOR_STEADY = 272
-GPSIMD_COLS = 0
+VECTOR_STEADY = 320
+SHORT_PIECE = 352
+SCALAR_LEAD = 3
+VECTOR_LEAD = 2
+RAW_BUFS = CHUNKS - 2
+LAST = CHUNKS - 1
 
 
 def tile_spatialcgnl_pb_t_e_kernel(tc, y, Wz_words, Wz_scales, gamma, beta, x, out):
@@ -41,13 +45,14 @@ def tile_spatialcgnl_pb_t_e_kernel(tc, y, Wz_words, Wz_scales, gamma, beta, x, o
 
     with ExitStack() as ctx:
         keep = ctx.enter_context(tc.tile_pool(name="keep", bufs=1))
-        raw_pool = ctx.enter_context(tc.tile_pool(name="raw", bufs=CHUNKS))
-        grouped_pool = ctx.enter_context(tc.tile_pool(name="grouped", bufs=3))
-        mx_pool = ctx.enter_context(tc.tile_pool(name="mx", bufs=3))
+        raw_pool = ctx.enter_context(tc.tile_pool(name="raw", bufs=RAW_BUFS))
+        grouped_pool = ctx.enter_context(tc.tile_pool(name="grouped", bufs=5))
+        mx_pool = ctx.enter_context(tc.tile_pool(name="mx", bufs=4))
         stat_pool = ctx.enter_context(tc.tile_pool(name="stat", bufs=4))
         wide_pool = ctx.enter_context(tc.tile_pool(name="wide", bufs=3))
+        result_pool = ctx.enter_context(tc.tile_pool(name="result", bufs=6))
         z_pool = ctx.enter_context(tc.psum_pool(name="z", bufs=3))
-        small_psum = ctx.enter_context(tc.psum_pool(name="small_psum", bufs=2))
+        small_psum = ctx.enter_context(tc.psum_pool(name="small_psum", bufs=1))
         ctx.enter_context(tc.manual_schedule())
 
         w_words = keep.tile([P, GROUPS * PASSES, 2 * P], U8, align_bytes=64)
@@ -65,17 +70,19 @@ def tile_spatialcgnl_pb_t_e_kernel(tc, y, Wz_words, Wz_scales, gamma, beta, x, o
         codes = {}
         scales = {}
         z = {}
+        parts = {}
         moments = {}
         totals = {}
         rstd = {}
+        within = {}
+        between = {}
         gain = {}
         neg_shift = {}
         neg_rest = {}
+        result = {}
 
-        def shares(i):
-            if i < EARLY_CHUNKS:
-                return VECTOR_EARLY, 0
-            return VECTOR_STEADY, 0
+        def vector_share(i):
+            return VECTOR_EARLY if i < EARLY_CHUNKS else VECTOR_STEADY
 
         def load_chunk(i):
             raw[i] = raw_pool.tile([P, PACK, POSITIONS], BF16, name="raw")
@@ -101,76 +108,81 @@ def tile_spatialcgnl_pb_t_e_kernel(tc, y, Wz_words, Wz_scales, gamma, beta, x, o
                 grouped[i] = grouped_pool.tile([P, POSITIONS, PACK], BF16, name="grouped", align_bytes=64)
             return grouped[i]
 
-        def regroup(copy, i, cols):
-            copy(
+        def regroup_vector(i):
+            cols = slice(0, vector_share(i))
+            nc.vector.tensor_copy(out=grouped_tile(i)[:, cols, :], in_=raw[i][:, :, cols].rearrange("p t n -> p n t"))
+
+        def regroup_scalar(i, first, end):
+            cols = slice(first, end)
+            nc.scalar.copy(
                 out=grouped_tile(i)[:, cols, :].rearrange("p (c r) t -> p c t r", r=RUN),
                 in_=raw[i][:, :, cols].rearrange("p t (c r) -> p c t r", r=RUN),
             )
 
-        def regroup_vector(i):
-            cols = slice(0, shares(i)[0])
-            nc.vector.tensor_copy(out=grouped_tile(i)[:, cols, :], in_=raw[i][:, :, cols].rearrange("p t n -> p n t"))
+        def quantise(i, cols):
+            if i not in codes:
+                codes[i] = mx_pool.tile([P, POSITIONS], U32, name="codes", align_bytes=64)
+                scales[i] = mx_pool.tile([P, POSITIONS], U8, name="scales", align_bytes=64)
+            nc.vector.quantize_mx(
+                out=codes[i][:, cols].bitcast(FP8X4),
+                scales=scales[i][:, cols],
+                in_=grouped[i][:, cols, :].rearrange("p n t -> p (n t)"),
+            )
 
-        def regroup_scalar(i, piece):
-            first = sum(shares(i))
-            middle = first + (POSITIONS - first) // 16 * 8
-            regroup(nc.scalar.copy, i, (slice(first, middle), slice(middle, POSITIONS))[piece])
-
-        def quantise_and_multiply(i):
+        def multiply(i, h):
             unit, k_pass = divmod(i, PASSES)
             slab = (unit % GROUPS) * PASSES + k_pass
-            codes[i] = mx_pool.tile([P, POSITIONS], U32, name="codes", align_bytes=64)
-            scales[i] = mx_pool.tile([P, POSITIONS], U8, name="scales", align_bytes=64)
-            nc.vector.quantize_mx(
-                out=codes[i][:].bitcast(FP8X4),
-                scales=scales[i][:],
-                in_=grouped[i][:].rearrange("p n t -> p (n t)"),
+            if unit not in z:
+                z[unit] = [z_pool.tile([P, BANK], F32, name="z%d" % half) for half in range(HALVES)]
+            cols = slice(h * BANK, (h + 1) * BANK)
+            nc.tensor.matmul_mx(
+                out=z[unit][h][:],
+                lhsT=w_words[:, slab, :].bitcast(FP4X4),
+                lhsT_scale=w_planes[:, slab, :],
+                rhs=codes[i][:, cols].bitcast(FP8X4),
+                rhs_scale=scales[i][:, cols],
+                start=(k_pass == 0),
+                stop=(k_pass == PASSES - 1),
             )
-            if k_pass == 0:
-                z[unit] = [z_pool.tile([P, BANK], F32, name="z%d" % h) for h in range(HALVES)]
-            for h in range(HALVES):
-                cols = slice(h * BANK, (h + 1) * BANK)
-                nc.tensor.matmul_mx(
-                    out=z[unit][h][:],
-                    lhsT=w_words[:, slab, :].bitcast(FP4X4),
-                    lhsT_scale=w_planes[:, slab, :],
-                    rhs=codes[i][:, cols].bitcast(FP8X4),
-                    rhs_scale=scales[i][:, cols],
-                    start=(k_pass == 0),
-                    stop=(k_pass == PASSES - 1),
-                )
 
-        def row_moments(unit):
-            parts = stat_pool.tile([P, HALVES, 6], F32, name="parts")
+        def quantise_and_multiply(i):
+            quantise(i, slice(0, POSITIONS))
             for h in range(HALVES):
-                nc.vector.bn_stats(out=parts[:, h, :], in_=z[unit][h][:])
+                multiply(i, h)
+
+        def half_moments(unit, h):
+            if unit not in parts:
+                parts[unit] = stat_pool.tile([P, HALVES, 6], F32, name="parts")
+            nc.vector.bn_stats(out=parts[unit][:, h, :], in_=z[unit][h][:])
+
+        def unit_mean(unit):
             moments[unit] = stat_pool.tile([P, 2], F32, name="moments")
-            nc.vector.bn_aggr(out=moments[unit][:], in_=parts[:].rearrange("p h s -> p (h s)"))
-            totals[unit] = small_psum.tile([P, 2], F32, name="totals", tag="small")
-            nc.tensor.matmul(
-                out=totals[unit][:, 0:1], lhsT=averager[:], rhs=moments[unit][:, 0:1], start=True, stop=True
-            )
+            nc.vector.bn_aggr(out=moments[unit][:], in_=parts[unit][:].rearrange("p h s -> p (h s)"))
+            totals[unit] = small_psum.tile([P, 2], F32, name="totals")
+            nc.tensor.matmul(out=totals[unit][:, 0:2], lhsT=averager[:], rhs=moments[unit][:], start=True, stop=True)
 
         def unit_variance(unit):
             square = stat_pool.tile([P, 1], F32, name="square")
             nc.scalar.activation(
                 out=square[:], in_=totals[unit][:, 0:1], func=ACT.Square, bias=moments[unit][:, 0:1], scale=-1.0
             )
-            nc.tensor.matmul(out=totals[unit][:, 1:2], lhsT=averager[:], rhs=square[:], start=True, stop=False)
-            nc.tensor.matmul(
-                out=totals[unit][:, 1:2], lhsT=averager[:], rhs=moments[unit][:, 1:2], start=False, stop=True
-            )
-
-        def inverse_deviation(unit):
-            rstd[unit] = stat_pool.tile([P, 1], F32, name="rstd")
-            nc.scalar.activation(
-                out=rstd[unit][:], in_=totals[unit][:, 1:2], func=ACT.Abs_reciprocal_sqrt, bias=EPS, scale=1.0
-            )
+            between[unit] = small_psum.tile([P, 1], F32, name="between")
+            nc.tensor.matmul(out=between[unit][:], lhsT=averager[:], rhs=square[:], start=True, stop=True)
+            within[unit] = stat_pool.tile([P, 1], F32, name="within")
+            nc.scalar.activation(out=within[unit][:], in_=totals[unit][:, 1:2], func=ACT.Identity, bias=EPS, scale=1.0)
 
         def channel_gain(unit):
             j = unit % GROUPS
+            rstd[unit] = stat_pool.tile([P, 1], F32, name="rstd")
+            nc.scalar.activation(
+                out=rstd[unit][:],
+                in_=between[unit][:],
+                func=ACT.Abs_reciprocal_sqrt,
+                bias=within[unit][:, 0:1],
+                scale=1.0,
+            )
             gain[unit] = stat_pool.tile([P, 1], F32, name="gain")
-            nc.vector.tensor_mul(out=gain[unit][:], in0=rstd[unit][:], in1=gamma_beta[:, j : j + 1])
+            nc.scalar.activation(out=gain[unit][:], in_=rstd[unit][:], func=ACT.Copy, scale=gamma_beta[:, j : j + 1])
 
         def channel_shift(unit):
             j = unit % GROUPS
@@ -183,36 +195,49 @@ def tile_spatialcgnl_pb_t_e_kernel(tc, y, Wz_words, Wz_scales, gamma, beta, x, o
                 op0=ALU.mult,
                 op1=ALU.subtract,
             )
-
-        def shift_residual(unit):
             neg_rest[unit] = wide_pool.tile([P, POSITIONS], F32, name="neg_rest")
-            nc.gpsimd.tensor_scalar(
-                out=neg_rest[unit][:],
-                in0=x_all[:, unit, :],
+
+        def shift_residual(tensor_scalar, unit, cols):
+            tensor_scalar(
+                out=neg_rest[unit][:, cols],
+                in0=x_all[:, unit, cols],
                 scalar1=-1.0,
                 scalar2=neg_shift[unit][:, 0:1],
                 op0=ALU.mult,
                 op1=ALU.add,
             )
 
-        def finish(unit):
-            result = wide_pool.tile([P, POSITIONS], F32, name="result")
-            for h in range(HALVES):
-                cols = slice(h * BANK, (h + 1) * BANK)
-                nc.vector.scalar_tensor_tensor(
-                    out=result[:, cols],
-                    in0=z[unit][h][:],
-                    scalar=gain[unit][:, 0:1],
-                    in1=neg_rest[unit][:, cols],
-                    op0=ALU.mult,
-                    op1=ALU.subtract,
-                )
-            nc.sync.dma_start(out=out_units[unit], in_=result[:])
+        def shift_residual_scalar(unit, cols):
+            nc.scalar.activation(
+                out=neg_rest[unit][:, cols],
+                in_=x_all[:, unit, cols],
+                func=ACT.Identity,
+                bias=neg_shift[unit][:, 0:1],
+                scale=-1.0,
+            )
+
+        def finish(unit, h, store):
+            if unit not in result:
+                result[unit] = result_pool.tile([P, POSITIONS], F32, name="result")
+            cols = slice(h * BANK, (h + 1) * BANK)
+            nc.vector.scalar_tensor_tensor(
+                out=result[unit][:, cols],
+                in0=z[unit][h][:],
+                scalar=gain[unit][:, 0:1],
+                in1=neg_rest[unit][:, cols],
+                op0=ALU.mult,
+                op1=ALU.subtract,
+            )
+            if store is not None:
+                nc.sync.dma_start(out=out_units[unit][:, store], in_=result[unit][:, store])
 
         def unpack_affine_rows():
-            columns = small_psum.tile([P, P], BF16, name="columns", tag="small")
+            columns = small_psum.tile([P, P], BF16, name="columns", tag="between")
             nc.tensor.transpose(out=columns[:], in_=affine_rows[:], identity=identity[:])
             nc.vector.tensor_copy(out=gamma_beta[:], in_=columns[:, 0 : 2 * GROUPS])
+
+        everything = slice(0, POSITIONS)
+        halves = (slice(0, BANK), slice(BANK, POSITIONS))
 
         nc.vector.memset(w_planes[:].rearrange("p g n -> p (g n)").bitcast(I32), 0)
         nc.vector.memset(affine_rows[:], 0.0)
@@ -225,40 +250,51 @@ def tile_spatialcgnl_pb_t_e_kernel(tc, y, Wz_words, Wz_scales, gamma, beta, x, o
         load_chunk(0)
         load_chunk(1)
         load_weights()
-        for i in range(2, CHUNKS):
+        for i in range(2, RAW_BUFS):
             load_chunk(i)
 
-        for i in range(2):
-            regroup_vector(i)
-            regroup_scalar(i, 0)
-            regroup_scalar(i, 1)
+        for i in range(SCALAR_LEAD):
+            if i < VECTOR_LEAD:
+                regroup_vector(i)
+            regroup_scalar(i, vector_share(i), POSITIONS)
+        for i in range(RAW_BUFS, CHUNKS):
+            load_chunk(i)
 
-        for step in range(CHUNKS + 3):
+        for step in range(CHUNKS):
             odd = step % 2 == 1
-            measured = (step - 1) // 2 if odd and step < CHUNKS else None
-            scaled = (step - 3) // 2 if odd and step >= 3 else None
-            finished = (step - 4) // 2 if not odd and step >= 4 else None
-            ahead = step + 2 if step + 2 < CHUNKS else None
-            if step < CHUNKS:
-                quantise_and_multiply(step)
-            if scaled is not None:
-                channel_gain(scaled)
-            if ahead is not None:
-                regroup_vector(ahead)
+            measured = (step - 1) // 2
+            if not odd and step >= 6:
+                finish((step - 6) // 2, 1, everything)
+            quantise_and_multiply(step)
+            if step + VECTOR_LEAD < CHUNKS:
+                regroup_vector(step + VECTOR_LEAD)
+            copied = step + SCALAR_LEAD
+            if not odd:
+                if copied < CHUNKS:
+                    regroup_scalar(copied, vector_share(copied), POSITIONS)
+                continue
             if step == 1:
                 unpack_affine_rows()
-            if scaled is not None:
-                channel_shift(scaled)
-                shift_residual(scaled)
-            if measured is not None:
-                row_moments(measured)
-            if finished is not None:
-                finish(finished)
-            if ahead is not None:
-                regroup_scalar(ahead, 0)
-            if measured is not None:
-                unit_variance(measured)
-            if ahead is not None:
-                regroup_scalar(ahead, 1)
-            if measured is not None:
-                inverse_deviation(measured)
+            if measured >= 2:
+                finish(measured - 2, 0, None)
+            if measured >= 1:
+                channel_shift(measured - 1)
+                shift_residual(nc.gpsimd.tensor_scalar, measured - 1, everything)
+            half_moments(measured, 0)
+            half_moments(measured, 1)
+            unit_mean(measured)
+            unit_variance(measured)
+            if copied < CHUNKS:
+                regroup_scalar(copied, vector_share(copied), vector_share(copied) + SHORT_PIECE)
+            channel_gain(measured)
+            if copied < CHUNKS:
+                regroup_scalar(copied, vector_share(copied) + SHORT_PIECE, POSITIONS)
+
+        finish(UNITS - 3, 1, everything)
+        finish(UNITS - 2, 0, halves[0])
+        finish(UNITS - 2, 1, halves[1])
+        channel_shift(UNITS - 1)
+        shift_residual(nc.vector.tensor_scalar, UNITS - 1, halves[0])
+        shift_residual_scalar(UNITS - 1, halves[1])
+        finish(UNITS - 1, 0, halves[0])
+        finish(UNITS - 1, 1, halves[1])

@@ -31,6 +31,7 @@ EARLY_CHUNKS = 4
 VECTOR_EARLY = 448
 VECTOR_STEADY = 320
 SHORT_PIECE = 352
+GAP_PIECE = 96
 SCALAR_LEAD = 3
 VECTOR_LEAD = 2
 RAW_BUFS = CHUNKS - 2
@@ -171,8 +172,7 @@ def tile_spatialcgnl_pb_t_e_kernel(tc, y, Wz_words, Wz_scales, gamma, beta, x, o
             within[unit] = stat_pool.tile([P, 1], F32, name="within")
             nc.scalar.activation(out=within[unit][:], in_=totals[unit][:, 1:2], func=ACT.Identity, bias=EPS, scale=1.0)
 
-        def channel_gain(unit):
-            j = unit % GROUPS
+        def inverse_deviation(unit):
             rstd[unit] = stat_pool.tile([P, 1], F32, name="rstd")
             nc.scalar.activation(
                 out=rstd[unit][:],
@@ -181,6 +181,9 @@ def tile_spatialcgnl_pb_t_e_kernel(tc, y, Wz_words, Wz_scales, gamma, beta, x, o
                 bias=within[unit][:, 0:1],
                 scale=1.0,
             )
+
+        def channel_gain(unit):
+            j = unit % GROUPS
             gain[unit] = stat_pool.tile([P, 1], F32, name="gain")
             nc.scalar.activation(out=gain[unit][:], in_=rstd[unit][:], func=ACT.Copy, scale=gamma_beta[:, j : j + 1])
 
@@ -263,8 +266,6 @@ def tile_spatialcgnl_pb_t_e_kernel(tc, y, Wz_words, Wz_scales, gamma, beta, x, o
         for step in range(CHUNKS):
             odd = step % 2 == 1
             measured = (step - 1) // 2
-            if not odd and step >= 6:
-                finish((step - 6) // 2, 1, everything)
             quantise_and_multiply(step)
             if step + VECTOR_LEAD < CHUNKS:
                 regroup_vector(step + VECTOR_LEAD)
@@ -282,15 +283,22 @@ def tile_spatialcgnl_pb_t_e_kernel(tc, y, Wz_words, Wz_scales, gamma, beta, x, o
                 shift_residual(nc.gpsimd.tensor_scalar, measured - 1, everything)
             half_moments(measured, 0)
             half_moments(measured, 1)
+            if 2 <= measured < UNITS - 1:
+                finish(measured - 2, 1, everything)
             unit_mean(measured)
+            if measured == UNITS - 1:
+                finish(measured - 2, 1, everything)
             unit_variance(measured)
+            first = vector_share(min(copied, LAST))
             if copied < CHUNKS:
-                regroup_scalar(copied, vector_share(copied), vector_share(copied) + SHORT_PIECE)
+                regroup_scalar(copied, first, first + SHORT_PIECE)
+            inverse_deviation(measured)
+            if copied < CHUNKS:
+                regroup_scalar(copied, first + SHORT_PIECE, first + SHORT_PIECE + GAP_PIECE)
             channel_gain(measured)
             if copied < CHUNKS:
-                regroup_scalar(copied, vector_share(copied) + SHORT_PIECE, POSITIONS)
+                regroup_scalar(copied, first + SHORT_PIECE + GAP_PIECE, POSITIONS)
 
-        finish(UNITS - 3, 1, everything)
         finish(UNITS - 2, 0, halves[0])
         finish(UNITS - 2, 1, halves[1])
         channel_shift(UNITS - 1)

@@ -29,7 +29,7 @@ FLOPS = 2 * UNITS * P * CHANNELS * POSITIONS
 RUN = 4
 EARLY_CHUNKS = 4
 VECTOR_EARLY = 448
-VECTOR_STEADY = 320
+VECTOR_STEADY = 352
 SHORT_PIECE = 352
 GAP_PIECE = 96
 SCALAR_LEAD = 3

@@ -111,7 +111,10 @@ def tile_spatialcgnl_pb_t_e_kernel(tc, y, Wz_words, Wz_scales, gamma, beta, x, o
 
         def regroup_vector(i):
             cols = slice(0, vector_share(i))
-            nc.vector.tensor_copy(out=grouped_tile(i)[:, cols, :], in_=raw[i][:, :, cols].rearrange("p t n -> p n t"))
+            nc.vector.tensor_copy(
+                out=grouped_tile(i)[:, cols, :].rearrange("p (c r) t -> p c t r", r=RUN),
+                in_=raw[i][:, :, cols].rearrange("p t (c r) -> p c t r", r=RUN),
+            )
 
         def regroup_scalar(i, first, end):
             cols = slice(first, end)

@@ -30,12 +30,18 @@ RUN = 4
 EARLY_CHUNKS = 4
 VECTOR_EARLY = 448
 VECTOR_STEADY = 352
+VECTOR_LAST = 128
 SHORT_PIECE = 352
 GAP_PIECE = 96
 SCALAR_LEAD = 3
 VECTOR_LEAD = 2
 RAW_BUFS = CHUNKS - 2
 LAST = CHUNKS - 1
+WARM_BEFORE = 4
+WARM_BETWEEN = 2
+WARM_AFTER = 3
+AFFINE_AFTER = 3
+RESIDUAL_AFTER = 4
 
 
 def tile_spatialcgnl_pb_t_e_kernel(tc, y, Wz_words, Wz_scales, gamma, beta, x, out):
@@ -50,7 +56,7 @@ def tile_spatialcgnl_pb_t_e_kernel(tc, y, Wz_words, Wz_scales, gamma, beta, x, o
         grouped_pool = ctx.enter_context(tc.tile_pool(name="grouped", bufs=5))
         mx_pool = ctx.enter_context(tc.tile_pool(name="mx", bufs=4))
         stat_pool = ctx.enter_context(tc.tile_pool(name="stat", bufs=4))
-        wide_pool = ctx.enter_context(tc.tile_pool(name="wide", bufs=3))
+        wide_pool = ctx.enter_context(tc.tile_pool(name="wide", bufs=4))
         result_pool = ctx.enter_context(tc.tile_pool(name="result", bufs=6))
         z_pool = ctx.enter_context(tc.psum_pool(name="z", bufs=3))
         small_psum = ctx.enter_context(tc.psum_pool(name="small_psum", bufs=1))
@@ -63,6 +69,7 @@ def tile_spatialcgnl_pb_t_e_kernel(tc, y, Wz_words, Wz_scales, gamma, beta, x, o
         identity = keep.tile([P, P], BF16)
         averager = keep.tile([P, P], F32)
         gamma_beta = keep.tile([P, 2 * GROUPS], F32)
+        neg_gamma = keep.tile([P, GROUPS], F32)
         one = keep.tile([P, 1], F32)
         table_warm = keep.tile([P, 1], F32)
 
@@ -81,16 +88,23 @@ def tile_spatialcgnl_pb_t_e_kernel(tc, y, Wz_words, Wz_scales, gamma, beta, x, o
         neg_shift = {}
         neg_rest = {}
         result = {}
+        centred = {}
+        unread = {}
 
         def vector_share(i):
+            if i == LAST:
+                return VECTOR_LAST
             return VECTOR_EARLY if i < EARLY_CHUNKS else VECTOR_STEADY
 
         def load_chunk(i):
             raw[i] = raw_pool.tile([P, PACK, POSITIONS], BF16, name="raw")
             nc.sync.dma_start(out=raw[i][:], in_=y_chunks[i])
-            if i % (GROUPS * PASSES) == GROUPS * PASSES - 1:
-                b = i // (GROUPS * PASSES)
-                nc.sync.dma_start(out=x_all[:, GROUPS * b : GROUPS * (b + 1), :], in_=x_images[b])
+            if i == AFFINE_AFTER:
+                nc.sync.dma_start(out=affine_rows[0:GROUPS, :], in_=gamma.rearrange("(j o) -> j o", j=GROUPS))
+                nc.sync.dma_start(out=affine_rows[GROUPS : 2 * GROUPS, :], in_=beta.rearrange("(j o) -> j o", j=GROUPS))
+            for b in range(IMAGES):
+                if i == min(GROUPS * PASSES * b + RESIDUAL_AFTER, LAST):
+                    nc.sync.dma_start(out=x_all[:, GROUPS * b : GROUPS * (b + 1), :], in_=x_images[b])
 
         def load_weights():
             nc.sync.dma_start(
@@ -165,13 +179,15 @@ def tile_spatialcgnl_pb_t_e_kernel(tc, y, Wz_words, Wz_scales, gamma, beta, x, o
             totals[unit] = small_psum.tile([P, 2], F32, name="totals")
             nc.tensor.matmul(out=totals[unit][:, 0:2], lhsT=averager[:], rhs=moments[unit][:], start=True, stop=True)
 
-        def unit_variance(unit):
+        def squared_offsets(unit):
             square = stat_pool.tile([P, 1], F32, name="square")
             nc.scalar.activation(
                 out=square[:], in_=totals[unit][:, 0:1], func=ACT.Square, bias=moments[unit][:, 0:1], scale=-1.0
             )
             between[unit] = small_psum.tile([P, 1], F32, name="between")
             nc.tensor.matmul(out=between[unit][:], lhsT=averager[:], rhs=square[:], start=True, stop=True)
+
+        def variance_within(unit):
             within[unit] = stat_pool.tile([P, 1], F32, name="within")
             nc.scalar.activation(out=within[unit][:], in_=totals[unit][:, 1:2], func=ACT.Identity, bias=EPS, scale=1.0)
 
@@ -213,15 +229,6 @@ def tile_spatialcgnl_pb_t_e_kernel(tc, y, Wz_words, Wz_scales, gamma, beta, x, o
                 op1=ALU.add,
             )
 
-        def shift_residual_scalar(unit, cols):
-            nc.scalar.activation(
-                out=neg_rest[unit][:, cols],
-                in_=x_all[:, unit, cols],
-                func=ACT.Identity,
-                bias=neg_shift[unit][:, 0:1],
-                scale=-1.0,
-            )
-
         def finish(unit, h, store):
             if unit not in result:
                 result[unit] = result_pool.tile([P, POSITIONS], F32, name="result")
@@ -237,10 +244,79 @@ def tile_spatialcgnl_pb_t_e_kernel(tc, y, Wz_words, Wz_scales, gamma, beta, x, o
             if store is not None:
                 nc.sync.dma_start(out=out_units[unit][:, store], in_=result[unit][:, store])
 
+        def keep_tensor_busy(i, passes, fresh):
+            if fresh:
+                unread[0] = small_psum.tile([P, BANK], F32, name="unread", tag="between")
+            slab = (i // PASSES % GROUPS) * PASSES + i % PASSES
+            for k in range(passes):
+                nc.tensor.matmul_mx(
+                    out=unread[0][:],
+                    lhsT=w_words[:, slab, :].bitcast(FP4X4),
+                    lhsT_scale=w_planes[:, slab, :],
+                    rhs=codes[i][:, 0:BANK].bitcast(FP8X4),
+                    rhs_scale=scales[i][:, 0:BANK],
+                    start=True,
+                    stop=True,
+                )
+
+        def shift_residual_scalar(unit, cols):
+            nc.scalar.activation(
+                out=neg_rest[unit][:, cols],
+                in_=x_all[:, unit, cols],
+                func=ACT.Identity,
+                bias=neg_shift[unit][:, 0:1],
+                scale=-1.0,
+            )
+
         def unpack_affine_rows():
             columns = small_psum.tile([P, P], BF16, name="columns", tag="between")
             nc.tensor.transpose(out=columns[:], in_=affine_rows[:], identity=identity[:])
             nc.vector.tensor_copy(out=gamma_beta[:], in_=columns[:, 0 : 2 * GROUPS])
+            nc.vector.tensor_scalar_mul(out=neg_gamma[:], in0=columns[:, 0:GROUPS], scalar1=-1.0)
+
+        def residual_plus_beta(unit, cols):
+            j = unit % GROUPS
+            if unit not in neg_rest:
+                neg_rest[unit] = wide_pool.tile([P, POSITIONS], F32, name="neg_rest")
+            nc.scalar.activation(
+                out=neg_rest[unit][:, cols],
+                in_=x_all[:, unit, cols],
+                func=ACT.Identity,
+                bias=gamma_beta[:, GROUPS + j : GROUPS + j + 1],
+                scale=1.0,
+            )
+
+        def centre_offset(unit):
+            j = unit % GROUPS
+            neg_shift[unit] = stat_pool.tile([P, 1], F32, name="neg_shift")
+            nc.scalar.activation(
+                out=neg_shift[unit][:], in_=totals[unit][:, 0:1], func=ACT.Copy, scale=neg_gamma[:, j : j + 1]
+            )
+            centred[unit] = wide_pool.tile([P, POSITIONS], F32, name="neg_rest")
+
+        def centre(unit, h):
+            j = unit % GROUPS
+            nc.scalar.activation(
+                out=centred[unit][:, h * BANK : (h + 1) * BANK],
+                in_=z[unit][h][:],
+                func=ACT.Identity,
+                bias=neg_shift[unit][:, 0:1],
+                scale=gamma_beta[:, j : j + 1],
+            )
+
+        def finish_centred(unit, h):
+            if unit not in result:
+                result[unit] = result_pool.tile([P, POSITIONS], F32, name="result")
+            cols = slice(h * BANK, (h + 1) * BANK)
+            nc.vector.scalar_tensor_tensor(
+                out=result[unit][:, cols],
+                in0=centred[unit][:, cols],
+                scalar=rstd[unit][:, 0:1],
+                in1=neg_rest[unit][:, cols],
+                op0=ALU.mult,
+                op1=ALU.add,
+            )
+            nc.sync.dma_start(out=out_units[unit][:, cols], in_=result[unit][:, cols])
 
         everything = slice(0, POSITIONS)
         halves = (slice(0, BANK), slice(BANK, POSITIONS))
@@ -249,8 +325,6 @@ def tile_spatialcgnl_pb_t_e_kernel(tc, y, Wz_words, Wz_scales, gamma, beta, x, o
         nc.vector.memset(affine_rows[:], 0.0)
         nc.vector.memset(one[:], 1.0)
         nc.vector.memset(averager[:], 1.0 / P)
-        nc.scalar.dma_start(out=affine_rows[0:GROUPS, :], in_=gamma.rearrange("(j o) -> j o", j=GROUPS))
-        nc.scalar.dma_start(out=affine_rows[GROUPS : 2 * GROUPS, :], in_=beta.rearrange("(j o) -> j o", j=GROUPS))
         nc.scalar.activation(out=table_warm[:], in_=one[:], func=ACT.Abs_reciprocal_sqrt)
         make_identity(nc, identity[:])
         load_chunk(0)
@@ -266,19 +340,24 @@ def tile_spatialcgnl_pb_t_e_kernel(tc, y, Wz_words, Wz_scales, gamma, beta, x, o
         for i in range(RAW_BUFS, CHUNKS):
             load_chunk(i)
 
-        for step in range(CHUNKS):
+        for step in range(LAST):
             odd = step % 2 == 1
             measured = (step - 1) // 2
             quantise_and_multiply(step)
-            if step + VECTOR_LEAD < CHUNKS:
+            if step == LAST - 2:
+                keep_tensor_busy(step, WARM_BEFORE, True)
+            if step == 1:
+                regroup_vector(2)
+            if 2 <= step < CHUNKS - VECTOR_LEAD:
                 regroup_vector(step + VECTOR_LEAD)
             copied = step + SCALAR_LEAD
             if not odd:
-                if copied < CHUNKS:
+                if copied < LAST:
                     regroup_scalar(copied, vector_share(copied), POSITIONS)
+                if copied == LAST:
+                    regroup_scalar(copied, vector_share(copied), BANK)
+                    regroup_scalar(copied, BANK, POSITIONS)
                 continue
-            if step == 1:
-                unpack_affine_rows()
             if measured >= 2:
                 finish(measured - 2, 0, None)
             if measured >= 1:
@@ -286,26 +365,52 @@ def tile_spatialcgnl_pb_t_e_kernel(tc, y, Wz_words, Wz_scales, gamma, beta, x, o
                 shift_residual(nc.gpsimd.tensor_scalar, measured - 1, everything)
             half_moments(measured, 0)
             half_moments(measured, 1)
-            if 2 <= measured < UNITS - 1:
+            if measured >= 2:
                 finish(measured - 2, 1, everything)
             unit_mean(measured)
-            if measured == UNITS - 1:
-                finish(measured - 2, 1, everything)
-            unit_variance(measured)
+            if step == LAST - 2:
+                keep_tensor_busy(step, WARM_BETWEEN, False)
+            if step == 1:
+                unpack_affine_rows()
+                regroup_vector(3)
+            squared_offsets(measured)
+            variance_within(measured)
             first = vector_share(min(copied, LAST))
             if copied < CHUNKS:
                 regroup_scalar(copied, first, first + SHORT_PIECE)
+            else:
+                residual_plus_beta(UNITS - 1, slice(0, BANK // 2))
             inverse_deviation(measured)
             if copied < CHUNKS:
                 regroup_scalar(copied, first + SHORT_PIECE, first + SHORT_PIECE + GAP_PIECE)
+            else:
+                residual_plus_beta(UNITS - 1, slice(BANK // 2, BANK))
             channel_gain(measured)
             if copied < CHUNKS:
                 regroup_scalar(copied, first + SHORT_PIECE + GAP_PIECE, POSITIONS)
+            else:
+                residual_plus_beta(UNITS - 1, halves[1])
 
-        finish(UNITS - 2, 0, halves[0])
-        finish(UNITS - 2, 1, halves[1])
-        channel_shift(UNITS - 1)
-        shift_residual(nc.vector.tensor_scalar, UNITS - 1, halves[0])
-        shift_residual_scalar(UNITS - 1, halves[1])
-        finish(UNITS - 1, 0, halves[0])
-        finish(UNITS - 1, 1, halves[1])
+        final = UNITS - 1
+        for h in range(HALVES):
+            quantise(LAST, halves[h])
+            multiply(LAST, h)
+        keep_tensor_busy(LAST, WARM_AFTER, True)
+        finish(final - 2, 0, None)
+        channel_shift(final - 1)
+        shift_residual_scalar(final - 1, everything)
+        half_moments(final, 0)
+        half_moments(final, 1)
+        unit_mean(final)
+        keep_tensor_busy(LAST, 1, False)
+        finish(final - 2, 1, everything)
+        squared_offsets(final)
+        centre_offset(final)
+        variance_within(final)
+        centre(final, 0)
+        inverse_deviation(final)
+        centre(final, 1)
+        finish(final - 1, 0, halves[0])
+        finish(final - 1, 1, halves[1])
+        finish_centred(final, 0)
+        finish_centred(final, 1)

@@ -28,6 +28,7 @@ FLOPS = 2 * UNITS * P * CHANNELS * POSITIONS
 
 RUN = 4
 EARLY_CHUNKS = 4
+VECTOR_FIRST = 672
 VECTOR_EARLY = 448
 VECTOR_STEADY = 352
 VECTOR_LAST = 128
@@ -92,6 +93,8 @@ def tile_spatialcgnl_pb_t_e_kernel(tc, y, Wz_words, Wz_scales, gamma, beta, x, o
         unread = {}
 
         def vector_share(i):
+            if i == 0:
+                return VECTOR_FIRST
             if i == LAST:
                 return VECTOR_LAST
             return VECTOR_EARLY if i < EARLY_CHUNKS else VECTOR_STEADY
@@ -304,10 +307,9 @@ def tile_spatialcgnl_pb_t_e_kernel(tc, y, Wz_words, Wz_scales, gamma, beta, x, o
                 scale=gamma_beta[:, j : j + 1],
             )
 
-        def finish_centred(unit, h):
+        def finish_centred(unit, cols):
             if unit not in result:
                 result[unit] = result_pool.tile([P, POSITIONS], F32, name="result")
-            cols = slice(h * BANK, (h + 1) * BANK)
             nc.vector.scalar_tensor_tensor(
                 out=result[unit][:, cols],
                 in0=centred[unit][:, cols],
@@ -371,8 +373,8 @@ def tile_spatialcgnl_pb_t_e_kernel(tc, y, Wz_words, Wz_scales, gamma, beta, x, o
             if step == LAST - 2:
                 keep_tensor_busy(step, WARM_BETWEEN, False)
             if step == 1:
-                unpack_affine_rows()
                 regroup_vector(3)
+                unpack_affine_rows()
             squared_offsets(measured)
             variance_within(measured)
             first = vector_share(min(copied, LAST))
@@ -412,5 +414,6 @@ def tile_spatialcgnl_pb_t_e_kernel(tc, y, Wz_words, Wz_scales, gamma, beta, x, o
         centre(final, 1)
         finish(final - 1, 0, halves[0])
         finish(final - 1, 1, halves[1])
-        finish_centred(final, 0)
-        finish_centred(final, 1)
+        finish_centred(final, halves[0])
+        finish_centred(final, slice(BANK, BANK + BANK // 2))
+        finish_centred(final, slice(BANK + BANK // 2, POSITIONS))

@@ -29,8 +29,9 @@ FLOPS = 2 * UNITS * P * CHANNELS * POSITIONS
 RUN = 4
 EARLY_CHUNKS = 4
 VECTOR_FIRST = 672
+VECTOR_SECOND = 576
 VECTOR_EARLY = 448
-VECTOR_STEADY = 352
+VECTOR_STEADY = 320
 VECTOR_LAST = 128
 SHORT_PIECE = 352
 GAP_PIECE = 96
@@ -93,8 +94,8 @@ def tile_spatialcgnl_pb_t_e_kernel(tc, y, Wz_words, Wz_scales, gamma, beta, x, o
         unread = {}
 
         def vector_share(i):
-            if i == 0:
-                return VECTOR_FIRST
+            if i < 2:
+                return (VECTOR_FIRST, VECTOR_SECOND)[i]
             if i == LAST:
                 return VECTOR_LAST
             return VECTOR_EARLY if i < EARLY_CHUNKS else VECTOR_STEADY
@@ -335,9 +336,8 @@ def tile_spatialcgnl_pb_t_e_kernel(tc, y, Wz_words, Wz_scales, gamma, beta, x, o
         for i in range(2, RAW_BUFS):
             load_chunk(i)
 
+        regroup_vector(0)
         for i in range(SCALAR_LEAD):
-            if i < VECTOR_LEAD:
-                regroup_vector(i)
             regroup_scalar(i, vector_share(i), POSITIONS)
         for i in range(RAW_BUFS, CHUNKS):
             load_chunk(i)
@@ -348,8 +348,8 @@ def tile_spatialcgnl_pb_t_e_kernel(tc, y, Wz_words, Wz_scales, gamma, beta, x, o
             quantise_and_multiply(step)
             if step == LAST - 2:
                 keep_tensor_busy(step, WARM_BEFORE, True)
-            if step == 1:
-                regroup_vector(2)
+            if step < 2:
+                regroup_vector(step + 1)
             if 2 <= step < CHUNKS - VECTOR_LEAD:
                 regroup_vector(step + VECTOR_LEAD)
             copied = step + SCALAR_LEAD

@@ -31,7 +31,7 @@ EARLY_CHUNKS = 4
 VECTOR_FIRST = 672
 VECTOR_SECOND = 576
 VECTOR_EARLY = 448
-VECTOR_STEADY = 320
+VECTOR_STEADY = 288
 VECTOR_LAST = 128
 SHORT_PIECE = 352
 GAP_PIECE = 96
@@ -39,6 +39,7 @@ SCALAR_LEAD = 3
 VECTOR_LEAD = 2
 RAW_BUFS = CHUNKS - 2
 LAST = CHUNKS - 1
+TENSOR_SHARE = 256
 WARM_BEFORE = 4
 WARM_BETWEEN = 2
 WARM_AFTER = 3
@@ -91,6 +92,7 @@ def tile_spatialcgnl_pb_t_e_kernel(tc, y, Wz_words, Wz_scales, gamma, beta, x, o
         neg_rest = {}
         result = {}
         centred = {}
+        turned = {}
         unread = {}
 
         def vector_share(i):
@@ -139,6 +141,30 @@ def tile_spatialcgnl_pb_t_e_kernel(tc, y, Wz_words, Wz_scales, gamma, beta, x, o
             nc.scalar.copy(
                 out=grouped_tile(i)[:, cols, :].rearrange("p (c r) t -> p c t r", r=RUN),
                 in_=raw[i][:, :, cols].rearrange("p t (c r) -> p c t r", r=RUN),
+            )
+
+        def tensor_regroups(i):
+            return i % 2 == 0 and 6 <= i < CHUNKS
+
+        def scalar_end(i):
+            return POSITIONS - TENSOR_SHARE if tensor_regroups(i) else POSITIONS
+
+        def regroup_tensor(i):
+            turned[i] = small_psum.tile([P, 2 * BANK], BF16, name="turned", tag="between")
+            for k in range(2):
+                first = POSITIONS - TENSOR_SHARE + k * (BANK // PACK)
+                nc.tensor.matmul(
+                    out=turned[i][:, k * BANK : (k + 1) * BANK],
+                    lhsT=identity[:],
+                    rhs=raw[i][:, :, first : first + BANK // PACK].rearrange("p t n -> p n t"),
+                    start=True,
+                    stop=True,
+                )
+
+        def take_regrouped(i):
+            nc.scalar.copy(
+                out=grouped_tile(i)[:, POSITIONS - TENSOR_SHARE : POSITIONS, :].rearrange("p n t -> p (n t)"),
+                in_=turned[i][:],
             )
 
         def quantise(i, cols):
@@ -346,6 +372,9 @@ def tile_spatialcgnl_pb_t_e_kernel(tc, y, Wz_words, Wz_scales, gamma, beta, x, o
             odd = step % 2 == 1
             measured = (step - 1) // 2
             quantise_and_multiply(step)
+            if tensor_regroups(step + SCALAR_LEAD):
+                regroup_tensor(step + SCALAR_LEAD)
+                take_regrouped(step + SCALAR_LEAD)
             if step == LAST - 2:
                 keep_tensor_busy(step, WARM_BEFORE, True)
             if step < 2:
@@ -389,8 +418,8 @@ def tile_spatialcgnl_pb_t_e_kernel(tc, y, Wz_words, Wz_scales, gamma, beta, x, o
                 residual_plus_beta(UNITS - 1, slice(BANK // 2, BANK))
             channel_gain(measured)
             if copied < CHUNKS:
-                regroup_scalar(copied, first + SHORT_PIECE + GAP_PIECE, POSITIONS)
-            else:
+                regroup_scalar(copied, first + SHORT_PIECE + GAP_PIECE, scalar_end(copied))
+            if copied >= CHUNKS:
                 residual_plus_beta(UNITS - 1, halves[1])
 
         final = UNITS - 1

@@ -40,6 +40,7 @@ VECTOR_LEAD = 2
 RAW_BUFS = CHUNKS - 2
 LAST = CHUNKS - 1
 TENSOR_SHARE = 256
+GPSIMD_SHARE = 96
 WARM_BEFORE = 4
 WARM_BETWEEN = 2
 WARM_AFTER = 3
@@ -146,8 +147,24 @@ def tile_spatialcgnl_pb_t_e_kernel(tc, y, Wz_words, Wz_scales, gamma, beta, x, o
         def tensor_regroups(i):
             return i % 2 == 0 and 6 <= i < CHUNKS
 
+        def gpsimd_regroups(i):
+            return tensor_regroups(i) and i >= 8
+
         def scalar_end(i):
+            if gpsimd_regroups(i):
+                return POSITIONS - TENSOR_SHARE - GPSIMD_SHARE
             return POSITIONS - TENSOR_SHARE if tensor_regroups(i) else POSITIONS
+
+        def regroup_gpsimd(i):
+            cols = slice(POSITIONS - TENSOR_SHARE - GPSIMD_SHARE, POSITIONS - TENSOR_SHARE)
+            nc.gpsimd.tensor_scalar(
+                out=grouped_tile(i)[:, cols, :],
+                in0=raw[i][:, :, cols].rearrange("p t n -> p n t"),
+                scalar1=1.0,
+                scalar2=0.0,
+                op0=ALU.mult,
+                op1=ALU.add,
+            )
 
         def regroup_tensor(i):
             turned[i] = small_psum.tile([P, 2 * BANK], BF16, name="turned", tag="between")
@@ -389,11 +406,13 @@ def tile_spatialcgnl_pb_t_e_kernel(tc, y, Wz_words, Wz_scales, gamma, beta, x, o
                     regroup_scalar(copied, vector_share(copied), BANK)
                     regroup_scalar(copied, BANK, POSITIONS)
                 continue
-            if measured >= 2:
-                finish(measured - 2, 0, None)
             if measured >= 1:
                 channel_shift(measured - 1)
                 shift_residual(nc.gpsimd.tensor_scalar, measured - 1, everything)
+            if gpsimd_regroups(copied):
+                regroup_gpsimd(copied)
+            if measured >= 2:
+                finish(measured - 2, 0, None)
             half_moments(measured, 0)
             half_moments(measured, 1)
             if measured >= 2:
@@ -407,8 +426,10 @@ def tile_spatialcgnl_pb_t_e_kernel(tc, y, Wz_words, Wz_scales, gamma, beta, x, o
             squared_offsets(measured)
             variance_within(measured)
             first = vector_share(min(copied, LAST))
+            if gpsimd_regroups(copied):
+                first -= GPSIMD_SHARE
             if copied < CHUNKS:
-                regroup_scalar(copied, first, first + SHORT_PIECE)
+                regroup_scalar(copied, vector_share(copied), first + SHORT_PIECE)
             else:
                 residual_plus_beta(UNITS - 1, slice(0, BANK // 2))
             inverse_deviation(measured)

from contextlib import ExitStack

import concourse.mybir as mybir
from concourse.masks import make_identity

F32 = mybir.dt.float32
BF16 = mybir.dt.bfloat16
I32 = mybir.dt.int32
U32 = mybir.dt.uint32
U8 = mybir.dt.uint8
FP8X4 = mybir.dt.float8_e4m3fn_x4
FP4X4 = mybir.dt.float4_e2m1fn_x4
ALU = mybir.AluOpType
ACT = mybir.ActivationFunctionType

P = 128
PACK = 4
K_PASS = P * PACK
IMAGES, GROUPS, CHANNELS, POSITIONS = 4, 2, 1024, 1024
UNITS = IMAGES * GROUPS
PASSES = CHANNELS // K_PASS
CHUNKS = UNITS * PASSES
BANK = 512
HALVES = POSITIONS // BANK
EPS = 1e-5

FLOPS = 2 * UNITS * P * CHANNELS * POSITIONS

RUN = 4
EARLY_CHUNKS = 4
VECTOR_FIRST = 672
VECTOR_SECOND = 576
VECTOR_EARLY = 448
VECTOR_STEADY = 288
VECTOR_LAST = 128
SHORT_PIECE = 352
GAP_PIECE = 96
SCALAR_LEAD = 3
VECTOR_LEAD = 2
RAW_BUFS = CHUNKS - 2
LAST = CHUNKS - 1
TENSOR_SHARE = 256
GPSIMD_SHARE = 96
WARM_BEFORE = 4
WARM_BETWEEN = 2
WARM_AFTER = 3
AFFINE_AFTER = 3
RESIDUAL_AFTER = 4


def tile_spatialcgnl_pb_t_e_kernel(tc, y, Wz_words, Wz_scales, gamma, beta, x, out):
    nc = tc.nc
    y_chunks = y.rearrange("b j (c p t) n -> (b j c) p t n", c=PASSES, p=P, t=PACK)
    x_images = x.rearrange("b (j o) h w -> b o j (h w)", j=GROUPS)
    out_units = out.rearrange("b (j o) h w -> (b j) o (h w)", j=GROUPS)

    with ExitStack() as ctx:
        keep = ctx.enter_context(tc.tile_pool(name="keep", bufs=1))
        raw_pool = ctx.enter_context(tc.tile_pool(name="raw", bufs=RAW_BUFS))
        grouped_pool = ctx.enter_context(tc.tile_pool(name="grouped", bufs=5))
        mx_pool = ctx.enter_context(tc.tile_pool(name="mx", bufs=4))
        stat_pool = ctx.enter_context(tc.tile_pool(name="stat", bufs=4))
        wide_pool = ctx.enter_context(tc.tile_pool(name="wide", bufs=4))
        result_pool = ctx.enter_context(tc.tile_pool(name="result", bufs=6))
        z_pool = ctx.enter_context(tc.psum_pool(name="z", bufs=3))
        small_psum = ctx.enter_context(tc.psum_pool(name="small_psum", bufs=1))
        ctx.enter_context(tc.manual_schedule())

        w_words = keep.tile([P, GROUPS * PASSES, 2 * P], U8, align_bytes=64)
        w_planes = keep.tile([P, GROUPS * PASSES, P], U8, align_bytes=64)
        x_all = keep.tile([P, UNITS, POSITIONS], BF16)
        affine_rows = keep.tile([P, P], BF16)
        identity = keep.tile([P, P], BF16)
        averager = keep.tile([P, P], F32)
        gamma_beta = keep.tile([P, 2 * GROUPS], F32)
        neg_gamma = keep.tile([P, GROUPS], F32)
        one = keep.tile([P, 1], F32)
        table_warm = keep.tile([P, 1], F32)

        raw = {}
        grouped = {}
        codes = {}
        scales = {}
        z = {}
        parts = {}
        moments = {}
        totals = {}
        rstd = {}
        within = {}
        between = {}
        gain = {}
        neg_shift = {}
        neg_rest = {}
        result = {}
        centred = {}
        turned = {}
        unread = {}

        def vector_share(i):
            if i < 2:
                return (VECTOR_FIRST, VECTOR_SECOND)[i]
            if i == LAST:
                return VECTOR_LAST
            return VECTOR_EARLY if i < EARLY_CHUNKS else VECTOR_STEADY

        def load_chunk(i):
            raw[i] = raw_pool.tile([P, PACK, POSITIONS], BF16, name="raw")
            nc.sync.dma_start(out=raw[i][:], in_=y_chunks[i])
            if i == AFFINE_AFTER:
                nc.sync.dma_start(out=affine_rows[0:GROUPS, :], in_=gamma.rearrange("(j o) -> j o", j=GROUPS))
                nc.sync.dma_start(out=affine_rows[GROUPS : 2 * GROUPS, :], in_=beta.rearrange("(j o) -> j o", j=GROUPS))
            for b in range(IMAGES):
                if i == min(GROUPS * PASSES * b + RESIDUAL_AFTER, LAST):
                    nc.sync.dma_start(out=x_all[:, GROUPS * b : GROUPS * (b + 1), :], in_=x_images[b])

        def load_weights():
            nc.sync.dma_start(
                out=w_words[:].bitcast(I32), in_=Wz_words.bitcast(I32).rearrange("g p n -> p g n")
            )
            for quadrant in range(4):
                nc.sync.dma_start(
                    out=w_planes[32 * quadrant : 32 * quadrant + 4].bitcast(I32),
                    in_=Wz_scales[:, 4 * quadrant : 4 * quadrant + 4, :]
                    .bitcast(I32)
                    .rearrange("g r n -> r g n"),
                )

        def grouped_tile(i):
            if i not in grouped:
                grouped[i] = grouped_pool.tile([P, POSITIONS, PACK], BF16, name="grouped", align_bytes=64)
            return grouped[i]

        def regroup_vector(i):
            cols = slice(0, vector_share(i))
            nc.vector.tensor_copy(
                out=grouped_tile(i)[:, cols, :].rearrange("p (c r) t -> p c t r", r=RUN),
                in_=raw[i][:, :, cols].rearrange("p t (c r) -> p c t r", r=RUN),
            )

        def regroup_scalar(i, first, end):
            cols = slice(first, end)
            nc.scalar.copy(
                out=grouped_tile(i)[:, cols, :].rearrange("p (c r) t -> p c t r", r=RUN),
                in_=raw[i][:, :, cols].rearrange("p t (c r) -> p c t r", r=RUN),
            )

        def tensor_regroups(i):
            return i % 2 == 0 and 6 <= i < CHUNKS

        def gpsimd_regroups(i):
            return tensor_regroups(i) and i >= 8

        def scalar_end(i):
            if gpsimd_regroups(i):
                return POSITIONS - TENSOR_SHARE - GPSIMD_SHARE
            return POSITIONS - TENSOR_SHARE if tensor_regroups(i) else POSITIONS

        def regroup_gpsimd(i):
            cols = slice(POSITIONS - TENSOR_SHARE - GPSIMD_SHARE, POSITIONS - TENSOR_SHARE)
            nc.gpsimd.tensor_scalar(
                out=grouped_tile(i)[:, cols, :],
                in0=raw[i][:, :, cols].rearrange("p t n -> p n t"),
                scalar1=1.0,
                scalar2=0.0,
                op0=ALU.mult,
                op1=ALU.add,
            )

        def regroup_tensor(i):
            turned[i] = small_psum.tile([P, 2 * BANK], BF16, name="turned", tag="between")
            for k in range(2):
                first = POSITIONS - TENSOR_SHARE + k * (BANK // PACK)
                nc.tensor.matmul(
                    out=turned[i][:, k * BANK : (k + 1) * BANK],
                    lhsT=identity[:],
                    rhs=raw[i][:, :, first : first + BANK // PACK].rearrange("p t n -> p n t"),
                    start=True,
                    stop=True,
                )

        def take_regrouped(i):
            nc.scalar.copy(
                out=grouped_tile(i)[:, POSITIONS - TENSOR_SHARE : POSITIONS, :].rearrange("p n t -> p (n t)"),
                in_=turned[i][:],
            )

        def quantise(i, cols):
            if i not in codes:
                codes[i] = mx_pool.tile([P, POSITIONS], U32, name="codes", align_bytes=64)
                scales[i] = mx_pool.tile([P, POSITIONS], U8, name="scales", align_bytes=64)
            nc.vector.quantize_mx(
                out=codes[i][:, cols].bitcast(FP8X4),
                scales=scales[i][:, cols],
                in_=grouped[i][:, cols, :].rearrange("p n t -> p (n t)"),
            )

        def multiply(i, h):
            unit, k_pass = divmod(i, PASSES)
            slab = (unit % GROUPS) * PASSES + k_pass
            if unit not in z:
                z[unit] = [z_pool.tile([P, BANK], F32, name="z%d" % half) for half in range(HALVES)]
            cols = slice(h * BANK, (h + 1) * BANK)
            nc.tensor.matmul_mx(
                out=z[unit][h][:],
                lhsT=w_words[:, slab, :].bitcast(FP4X4),
                lhsT_scale=w_planes[:, slab, :],
                rhs=codes[i][:, cols].bitcast(FP8X4),
                rhs_scale=scales[i][:, cols],
                start=(k_pass == 0),
                stop=(k_pass == PASSES - 1),
            )

        def quantise_and_multiply(i):
            quantise(i, slice(0, POSITIONS))
            for h in range(HALVES):
                multiply(i, h)

        def half_moments(unit, h):
            if unit not in parts:
                parts[unit] = stat_pool.tile([P, HALVES, 6], F32, name="parts")
            nc.vector.bn_stats(out=parts[unit][:, h, :], in_=z[unit][h][:])

        def unit_mean(unit):
            moments[unit] = stat_pool.tile([P, 2], F32, name="moments")
            nc.vector.bn_aggr(out=moments[unit][:], in_=parts[unit][:].rearrange("p h s -> p (h s)"))
            totals[unit] = small_psum.tile([P, 2], F32, name="totals")
            nc.tensor.matmul(out=totals[unit][:, 0:2], lhsT=averager[:], rhs=moments[unit][:], start=True, stop=True)

        def squared_offsets(unit):
            square = stat_pool.tile([P, 1], F32, name="square")
            nc.scalar.activation(
                out=square[:], in_=totals[unit][:, 0:1], func=ACT.Square, bias=moments[unit][:, 0:1], scale=-1.0
            )
            between[unit] = small_psum.tile([P, 1], F32, name="between")
            nc.tensor.matmul(out=between[unit][:], lhsT=averager[:], rhs=square[:], start=True, stop=True)

        def variance_within(unit):
            within[unit] = stat_pool.tile([P, 1], F32, name="within")
            nc.scalar.activation(out=within[unit][:], in_=totals[unit][:, 1:2], func=ACT.Identity, bias=EPS, scale=1.0)

        def inverse_deviation(unit):
            rstd[unit] = stat_pool.tile([P, 1], F32, name="rstd")
            nc.scalar.activation(
                out=rstd[unit][:],
                in_=between[unit][:],
                func=ACT.Abs_reciprocal_sqrt,
                bias=within[unit][:, 0:1],
                scale=1.0,
            )

        def channel_gain(unit):
            j = unit % GROUPS
            gain[unit] = stat_pool.tile([P, 1], F32, name="gain")
            nc.scalar.activation(out=gain[unit][:], in_=rstd[unit][:], func=ACT.Copy, scale=gamma_beta[:, j : j + 1])

        def channel_shift(unit):
            j = unit % GROUPS
            neg_shift[unit] = stat_pool.tile([P, 1], F32, name="neg_shift")
            nc.vector.tensor_scalar(
                out=neg_shift[unit][:],
                in0=totals[unit][:, 0:1],
                scalar1=gain[unit][:, 0:1],
                scalar2=gamma_beta[:, GROUPS + j : GROUPS + j + 1],
                op0=ALU.mult,
                op1=ALU.subtract,
            )
            neg_rest[unit] = wide_pool.tile([P, POSITIONS], F32, name="neg_rest")

        def shift_residual(tensor_scalar, unit, cols):
            tensor_scalar(
                out=neg_rest[unit][:, cols],
                in0=x_all[:, unit, cols],
                scalar1=-1.0,
                scalar2=neg_shift[unit][:, 0:1],
                op0=ALU.mult,
                op1=ALU.add,
            )

        def finish(unit, h, store):
            if unit not in result:
                result[unit] = result_pool.tile([P, POSITIONS], F32, name="result")
            cols = slice(h * BANK, (h + 1) * BANK)
            nc.vector.scalar_tensor_tensor(
                out=result[unit][:, cols],
                in0=z[unit][h][:],
                scalar=gain[unit][:, 0:1],
                in1=neg_rest[unit][:, cols],
                op0=ALU.mult,
                op1=ALU.subtract,
            )
            if store is not None:
                nc.sync.dma_start(out=out_units[unit][:, store], in_=result[unit][:, store])

        def keep_tensor_busy(i, passes, fresh):
            if fresh:
                unread[0] = small_psum.tile([P, BANK], F32, name="unread", tag="between")
            slab = (i // PASSES % GROUPS) * PASSES + i % PASSES
            for k in range(passes):
                nc.tensor.matmul_mx(
                    out=unread[0][:],
                    lhsT=w_words[:, slab, :].bitcast(FP4X4),
                    lhsT_scale=w_planes[:, slab, :],
                    rhs=codes[i][:, 0:BANK].bitcast(FP8X4),
                    rhs_scale=scales[i][:, 0:BANK],
                    start=True,
                    stop=True,
                )

        def shift_residual_scalar(unit, cols):
            nc.scalar.activation(
                out=neg_rest[unit][:, cols],
                in_=x_all[:, unit, cols],
                func=ACT.Identity,
                bias=neg_shift[unit][:, 0:1],
                scale=-1.0,
            )

        def unpack_affine_rows():
            columns = small_psum.tile([P, P], BF16, name="columns", tag="between")
            nc.tensor.transpose(out=columns[:], in_=affine_rows[:], identity=identity[:])
            nc.vector.tensor_copy(out=gamma_beta[:], in_=columns[:, 0 : 2 * GROUPS])
            nc.vector.tensor_scalar_mul(out=neg_gamma[:], in0=columns[:, 0:GROUPS], scalar1=-1.0)

        def residual_plus_beta(unit, cols):
            j = unit % GROUPS
            if unit not in neg_rest:
                neg_rest[unit] = wide_pool.tile([P, POSITIONS], F32, name="neg_rest")
            nc.scalar.activation(
                out=neg_rest[unit][:, cols],
                in_=x_all[:, unit, cols],
                func=ACT.Identity,
                bias=gamma_beta[:, GROUPS + j : GROUPS + j + 1],
                scale=1.0,
            )

        def centre_offset(unit):
            j = unit % GROUPS
            neg_shift[unit] = stat_pool.tile([P, 1], F32, name="neg_shift")
            nc.scalar.activation(
                out=neg_shift[unit][:], in_=totals[unit][:, 0:1], func=ACT.Copy, scale=neg_gamma[:, j : j + 1]
            )
            centred[unit] = wide_pool.tile([P, POSITIONS], F32, name="neg_rest")

        def centre(unit, h):
            j = unit % GROUPS
            nc.scalar.activation(
                out=centred[unit][:, h * BANK : (h + 1) * BANK],
                in_=z[unit][h][:],
                func=ACT.Identity,
                bias=neg_shift[unit][:, 0:1],
                scale=gamma_beta[:, j : j + 1],
            )

        def finish_centred(unit, cols):
            if unit not in result:
                result[unit] = result_pool.tile([P, POSITIONS], F32, name="result")
            nc.vector.scalar_tensor_tensor(
                out=result[unit][:, cols],
                in0=centred[unit][:, cols],
                scalar=rstd[unit][:, 0:1],
                in1=neg_rest[unit][:, cols],
                op0=ALU.mult,
                op1=ALU.add,
            )
            nc.sync.dma_start(out=out_units[unit][:, cols], in_=result[unit][:, cols])

        everything = slice(0, POSITIONS)
        halves = (slice(0, BANK), slice(BANK, POSITIONS))

        nc.vector.memset(w_planes[:].rearrange("p g n -> p (g n)").bitcast(I32), 0)
        nc.vector.memset(affine_rows[:], 0.0)
        nc.vector.memset(one[:], 1.0)
        nc.vector.memset(averager[:], 1.0 / P)
        nc.scalar.activation(out=table_warm[:], in_=one[:], func=ACT.Abs_reciprocal_sqrt)
        make_identity(nc, identity[:])
        load_chunk(0)
        load_chunk(1)
        load_weights()
        for i in range(2, RAW_BUFS):
            load_chunk(i)

        regroup_vector(0)
        for i in range(SCALAR_LEAD):
            regroup_scalar(i, vector_share(i), POSITIONS)
        for i in range(RAW_BUFS, CHUNKS):
            load_chunk(i)

        for step in range(LAST):
            odd = step % 2 == 1
            measured = (step - 1) // 2
            quantise_and_multiply(step)
            if tensor_regroups(step + SCALAR_LEAD):
                regroup_tensor(step + SCALAR_LEAD)
                take_regrouped(step + SCALAR_LEAD)
            if step == LAST - 2:
                keep_tensor_busy(step, WARM_BEFORE, True)
            if step < 2:
                regroup_vector(step + 1)
            if 2 <= step < CHUNKS - VECTOR_LEAD:
                regroup_vector(step + VECTOR_LEAD)
            copied = step + SCALAR_LEAD
            if not odd:
                if copied < LAST:
                    regroup_scalar(copied, vector_share(copied), POSITIONS)
                if copied == LAST:
                    regroup_scalar(copied, vector_share(copied), BANK)
                    regroup_scalar(copied, BANK, POSITIONS)
                continue
            if measured >= 1:
                channel_shift(measured - 1)
                shift_residual(nc.gpsimd.tensor_scalar, measured - 1, everything)
            if gpsimd_regroups(copied):
                regroup_gpsimd(copied)
            if measured >= 2:
                finish(measured - 2, 0, None)
            half_moments(measured, 0)
            half_moments(measured, 1)
            if measured >= 2:
                finish(measured - 2, 1, everything)
            unit_mean(measured)
            if step == LAST - 2:
                keep_tensor_busy(step, WARM_BETWEEN, False)
            if step == 1:
                regroup_vector(3)
                unpack_affine_rows()
            squared_offsets(measured)
            variance_within(measured)
            first = vector_share(min(copied, LAST))
            if gpsimd_regroups(copied):
                first -= GPSIMD_SHARE
            if copied < CHUNKS:
                regroup_scalar(copied, vector_share(copied), first + SHORT_PIECE)
            else:
                residual_plus_beta(UNITS - 1, slice(0, BANK // 2))
            inverse_deviation(measured)
            if copied < CHUNKS:
                regroup_scalar(copied, first + SHORT_PIECE, first + SHORT_PIECE + GAP_PIECE)
            else:
                residual_plus_beta(UNITS - 1, slice(BANK // 2, BANK))
            channel_gain(measured)
            if copied < CHUNKS:
                regroup_scalar(copied, first + SHORT_PIECE + GAP_PIECE, scalar_end(copied))
            if copied >= CHUNKS:
                residual_plus_beta(UNITS - 1, halves[1])

        final = UNITS - 1
        for h in range(HALVES):
            quantise(LAST, halves[h])
            multiply(LAST, h)
        keep_tensor_busy(LAST, WARM_AFTER, True)
        finish(final - 2, 0, None)
        channel_shift(final - 1)
        shift_residual_scalar(final - 1, everything)
        half_moments(final, 0)
        half_moments(final, 1)
        unit_mean(final)
        keep_tensor_busy(LAST, 1, False)
        finish(final - 2, 1, everything)
        squared_offsets(final)
        centre_offset(final)
        variance_within(final)
        centre(final, 0)
        inverse_deviation(final)
        centre(final, 1)
        finish(final - 1, 0, halves[0])
        finish(final - 1, 1, halves[1])
        finish_centred(final, halves[0])
        finish_centred(final, slice(BANK, BANK + BANK // 2))
        finish_centred(final, slice(BANK + BANK // 2, POSITIONS))
